import numpy as np
import ml_dtypes


def mxq(x, axis, fmt="e4m3"):
    dtype, down = {"e4m3": (ml_dtypes.float8_e4m3fn, 7), "e5m2": (ml_dtypes.float8_e5m2, 14)}[fmt]
    v = np.moveaxis(np.asarray(x, np.float32).astype(ml_dtypes.bfloat16).astype(np.float64), axis, -1)
    blocks = v.reshape(v.shape[:-1] + (-1, 32))
    amax = np.abs(blocks).max(-1, keepdims=True)
    byte = np.maximum(np.where(amax > 0, np.frexp(amax)[1] - 1 + 127, 0) - down, 1)
    scale = np.exp2(byte - 127.0)
    codes = (blocks / scale).astype(np.float32).astype(dtype).astype(np.float64)
    return np.moveaxis((codes * scale).reshape(v.shape), -1, axis)


BF16 = ml_dtypes.bfloat16


def bf(x):
    return np.asarray(x, np.float32).astype(BF16)


def f64(x):
    return np.asarray(x).astype(np.float64)


N, CK, CV, T, H, W = 2, 128, 512, 4, 32, 32
Q = H * W
M = T * Q


def setup_inputs():
    return {"q_key": bf(np.random.standard_normal((N, CK, H, W))),
            "q_val": bf(np.random.standard_normal((N, CV, H, W))),
            "m_key": bf(np.random.standard_normal((N, CK, T, H, W))),
            "m_val": bf(np.random.standard_normal((N, CV, T, H, W)) * 0.5 * Q / np.sqrt(M))}


def reference(q_key, q_val, m_key, m_val):
    qk = f64(q_key).reshape(N, CK, Q)
    mk = f64(m_key).reshape(N, CK, M)
    aff = (qk.transpose(0, 2, 1) @ mk) * (CK ** -0.5)
    e = np.exp(aff - aff.max(axis=1, keepdims=True))
    attn = e / e.sum(axis=1, keepdims=True)
    mv = f64(m_val).reshape(N, CV, M)
    mapped = (mxq(mv, 2, "e4m3") @ mxq(attn, 2, "e4m3").transpose(0, 2, 1)).reshape(N, CV, H, W)
    return np.concatenate([f64(q_val), mapped], axis=1)

@@ -1,0 +1,409 @@
+from contextlib import ExitStack
+
+import concourse.mybir as mybir
+from concourse.masks import make_identity
+
+F32 = mybir.dt.float32
+BF16 = mybir.dt.bfloat16
+U32 = mybir.dt.uint32
+U8 = mybir.dt.uint8
+FP8X4 = mybir.dt.float8_e4m3fn_x4
+ALU = mybir.AluOpType
+ACT = mybir.ActivationFunctionType
+
+P = 128
+NS = 2
+CV = 512
+Q = 1024
+M = 4096
+HALF = 512
+PASSES = 8
+ROUNDS = NS * PASSES
+STEPS = 2 * ROUNDS
+NAFF = 4 * STEPS
+RING = 3
+SCALE = 128.0 ** -0.5
+FLOPS = 2 * NS * Q * M * (128 + CV)
+
+MANUAL = True
+GQ = 224
+VQ = 64
+HEAD_CASTS = 5
+SLOTS = 11
+
+
+def split_of(rho):
+    if rho == ROUNDS - 1:
+        return {"G": [(512, 800)], "S": [(384, 512), (800, 1024)], "V": [(0, 384)]}
+    if rho == ROUNDS - 2:
+        return {"G": [(0, GQ), (GQ, 2 * GQ)], "S": [(2 * GQ + VQ, 1024)], "V": [(2 * GQ, 2 * GQ + VQ)]}
+    return {"G": [(0, GQ), (GQ, 2 * GQ)], "S": [(2 * GQ + VQ, 1024)], "V": [(2 * GQ, 2 * GQ + VQ)]}
+
+
+def tile_stm_head_kernel(tc, q_key, q_val, m_key, m_val, out):
+    nc = tc.nc
+    qk_src = [q_key[n].rearrange("c h w -> c (h w)") for n in range(NS)]
+    mk_src = [m_key[n].rearrange("c t h w -> c (t h w)") for n in range(NS)]
+    mv_src = [m_val[n].rearrange("(j c) t h w -> c j (t h w)", c=P) for n in range(NS)]
+    qv_src = [q_val[n].rearrange("(j c) h w -> c j (h w)", c=P) for n in range(NS)]
+    out_v = [out[n].rearrange("(j c) h w -> c j (h w)", c=P) for n in range(NS)]
+
+    with ExitStack() as ctx:
+        const = ctx.enter_context(tc.tile_pool(name="const", bufs=1))
+        raws = ctx.enter_context(tc.tile_pool(name="raws", bufs=2))
+        work = ctx.enter_context(tc.tile_pool(name="work", bufs=2))
+        keep = ctx.enter_context(tc.tile_pool(name="keep", bufs=SLOTS))
+        small = ctx.enter_context(tc.tile_pool(name="small", bufs=4))
+        psum = ctx.enter_context(tc.psum_pool(name="psum", bufs=1))
+        if MANUAL:
+            ctx.enter_context(tc.manual_schedule())
+
+        ident = const.tile([P, P], F32)
+        make_identity(nc, ident[:])
+
+        qk = {}
+        mk = {}
+        mvraw = {}
+        ring = {}
+        e_t = {}
+        m_first = {}
+        m_all = {}
+        sums = {}
+        recs = {}
+        grouped = {}
+        staged = {}
+        a_codes = {}
+        a_scales = {}
+        gmv = {}
+        v_codes = {}
+        v_scales = {}
+        tps = {}
+        acc = {}
+        qv_b = {}
+        qv_f = {}
+        stores = {}
+
+        def load_qk(n):
+            t = const.tile([P, Q], BF16, name="qk%d" % n)
+            nc.sync.dma_start(out=t[:], in_=qk_src[n])
+            qk[n] = t
+
+        def load_mk(n, quarter):
+            t = const.tile([P, 1024], BF16, name="mk%d_%d" % (n, quarter))
+            nc.sync.dma_start(out=t[:], in_=mk_src[n][:, 1024 * quarter : 1024 * quarter + 1024])
+            mk[(n, quarter)] = t
+
+        def load_mv(chunk):
+            n = chunk // 4
+            col = 1024 * (chunk % 4)
+            mv_raw = raws.tile([P, 4, 1024], BF16, tag="mvraw")
+            nc.sync.dma_start(out=mv_raw[:], in_=mv_src[n][:, :, col : col + 1024])
+            mvraw[chunk] = mv_raw
+
+        def load_qv(k):
+            qvb = raws.tile([P, Q], BF16, tag="qvb", bufs=3)
+            nc.sync.dma_start(out=qvb[:], in_=qv_src[k // 4][:, k % 4, :])
+            qv_b[k] = qvb
+
+        def aff(c):
+            s, k = divmod(c, 4)
+            r, w = divmod(s, 2)
+            n, g = divmod(r, PASSES)
+            e, h = k % 2, k // 2
+            base = 512 * (g % 2) + 256 * w
+            ps = psum.tile([P, HALF], F32, tag="ring%d" % (c % RING))
+            nc.tensor.matmul(
+                out=ps[:],
+                lhsT=mk[(n, g // 2)][:, base + e : base + 256 : 2],
+                rhs=qk[n][:, HALF * h : HALF * h + HALF],
+                start=True,
+                stop=True,
+            )
+            ring[c] = ps
+
+        def shift_out(c):
+            s, k = divmod(c, 4)
+            r, w = divmod(s, 2)
+            e, h = k % 2, k // 2
+            t = 2 * w + e
+            if r not in e_t:
+                ez = work.tile([P, 4, Q], F32, tag="ez", bufs=3)
+                e_t[r] = ez
+            dst = e_t[r][:, t, HALF * h : HALF * h + HALF]
+            if h == 0:
+                mf = small.tile([P, 1], F32, tag="mf")
+                m_first[(r, t)] = mf
+                nc.vector.tensor_scalar(
+                    out=dst, in0=ring[c][:], scalar1=-SCALE, scalar2=None, op0=ALU.mult, op1=ALU.min, accum_out=mf[:]
+                )
+            else:
+                ma = small.tile([P, 1], F32, tag="ma", bufs=8)
+                m_all[(r, t)] = ma
+                nc.vector.tensor_scalar(
+                    out=dst,
+                    in0=ring[c][:],
+                    scalar1=-SCALE,
+                    scalar2=m_first[(r, t)][:],
+                    op0=ALU.mult,
+                    op1=ALU.min,
+                    accum_out=ma[:],
+                )
+
+        def exp_tile(r, t):
+            if r not in sums:
+                sm = small.tile([P, 4], F32, tag="sm")
+                sums[r] = sm
+            nc.scalar.activation(
+                out=e_t[r][:, t, :],
+                in_=e_t[r][:, t, :],
+                func=ACT.Exp,
+                bias=m_all[(r, t)][:],
+                scale=-1.0,
+                accum_out=sums[r][:, t : t + 1],
+            )
+
+        def recip(r):
+            rc = small.tile([P, 4], F32, tag="rc")
+            nc.vector.reciprocal(out=rc[:], in_=sums[r][:])
+            recs[r] = rc
+            gr = work.tile([P, Q, 4], BF16, tag="gr", align_bytes=64)
+            grouped[r] = gr
+
+        def direct(eng, r, q0, q1, rc):
+            eng.tensor_tensor(
+                out=grouped[r][:, q0:q1, :],
+                in0=e_t[r][:, :, q0:q1].rearrange("p t q -> p q t"),
+                in1=rc[:].unsqueeze(1).to_broadcast([P, q1 - q0, 4]),
+                op=ALU.mult,
+            )
+
+        def second_piece(r):
+            rc2 = small.tile([P, 4], F32, tag="rc2")
+            nc.vector.tensor_copy(out=rc2[:], in_=recs[r][:])
+            q0, q1 = split_of(r)["G"][1]
+            direct(nc.gpsimd, r, q0, q1, rc2)
+
+        def stage(r, i, ts):
+            q0, q1 = split_of(r)["S"][i]
+            if (r, i) not in staged:
+                ab = work.tile([P, 4, 512], BF16, tag="ab")
+                staged[(r, i)] = ab
+            for t in ts:
+                nc.scalar.activation(
+                    out=staged[(r, i)][:, t, 0 : q1 - q0],
+                    in_=e_t[r][:, t, q0:q1],
+                    func=ACT.Copy,
+                    scale=recs[r][:, t : t + 1],
+                )
+
+        def regroup(r, i):
+            q0, q1 = split_of(r)["S"][i]
+            nc.vector.tensor_copy(
+                out=grouped[r][:, q0:q1, :].rearrange("p (c i) t -> p c t i", i=4),
+                in_=staged[(r, i)][:, :, 0 : q1 - q0].rearrange("p t (c i) -> p c t i", i=4),
+            )
+
+        def quantise_attn(r, q0, q1):
+            if r not in a_codes:
+                ac = keep.tile([P, Q], U32, tag="ac", align_bytes=64)
+                asc = keep.tile([P, Q], U8, tag="asc", align_bytes=64)
+                a_codes[r] = ac
+                a_scales[r] = asc
+            nc.vector.quantize_mx(
+                out=a_codes[r][:, q0:q1].bitcast(FP8X4),
+                scales=a_scales[r][:, q0:q1],
+                in_=grouped[r][:, q0:q1, :].rearrange("p q t -> p (q t)"),
+            )
+
+        def mv_transposes(r, b):
+            rawf = mvraw[r // 2][:].bitcast(F32)
+            tp = psum.tile([P, 2, 2, P], F32, tag="tp")
+            for jj in range(2):
+                for u in range(2):
+                    w0 = 256 * (r % 2) + 128 * u
+                    nc.tensor.transpose(tp[:, jj, u, :], rawf[:, 2 * b + jj, w0 : w0 + 128], ident[:])
+            tps[(r, b)] = tp
+
+        def mv_copy(r, b):
+            if r not in gmv:
+                gm = work.tile([P, 4 * CV], BF16, tag="gmv", align_bytes=64)
+                gmv[r] = gm
+            words = gmv[r][:].bitcast(F32).rearrange("p (j c u) -> p j c u", j=4, u=2)
+            nc.scalar.copy(out=words[:, 2 * b : 2 * b + 2], in_=tps[(r, b)][:].rearrange("p j u c -> p j c u"))
+
+        def quantise_mv(r):
+            vc = keep.tile([P, CV], U32, tag="vc", align_bytes=64)
+            vs = keep.tile([P, CV], U8, tag="vs", align_bytes=64)
+            nc.vector.quantize_mx(out=vc[:].bitcast(FP8X4), scales=vs[:], in_=gmv[r][:])
+            v_codes[r] = vc
+            v_scales[r] = vs
+
+        def mx(n, h, g, j, tag):
+            r = PASSES * n + g
+            if g == 0:
+                a = psum.tile([P, HALF], F32, tag=tag)
+                acc[(n, h, j)] = a
+            nc.tensor.matmul_mx(
+                out=acc[(n, h, j)][:],
+                lhsT=v_codes[r][:, P * j : P * j + P].bitcast(FP8X4),
+                lhsT_scale=v_scales[r][:, P * j : P * j + P],
+                rhs=a_codes[r][:, HALF * h : HALF * h + HALF].bitcast(FP8X4),
+                rhs_scale=a_scales[r][:, HALF * h : HALF * h + HALF],
+                start=(g == 0),
+                stop=(g == PASSES - 1),
+            )
+
+        def leave(eng_name, n, h, j):
+            ost = work.tile([P, HALF], F32, tag="ost", bufs=4)
+            if eng_name == "S":
+                nc.scalar.copy(out=ost[:], in_=acc[(n, h, j)][:])
+            else:
+                nc.vector.tensor_copy(out=ost[:], in_=acc[(n, h, j)][:])
+            stores["due"].append((out_v[n][:, 4 + j, HALF * h : HALF * h + HALF], ost))
+
+        def cast_qv(k):
+            qvf = raws.tile([P, Q], F32, tag="qvf")
+            nc.gpsimd.tensor_scalar(out=qvf[:], in0=qv_b[k][:], scalar1=1.0, scalar2=0.0, op0=ALU.mult, op1=ALU.add)
+            stores["due"].append((out_v[k // 4][:, k % 4, :], qvf))
+
+        def flush_stores():
+            for dst, src in stores["due"]:
+                nc.sync.dma_start(out=dst, in_=src[:])
+            stores["due"] = []
+
+        LATE = ["ring0", "ring1", "ring2", "tp"]
+
+        def pe_extras(s):
+            jobs = []
+            if s < STEPS:
+                jobs.append(("T", s // 2, s % 2))
+            if s >= 6 and s % 2 == 0 and (s - 6) // 2 < PASSES:
+                jobs.extend([("X", 0, 0, (s - 6) // 2, j, "acc%d" % j) for j in range(4)])
+            if 21 <= s < 25:
+                jobs.extend([("X", 0, 1, g, s - 21, "acc%d" % (s - 21)) for g in range(PASSES)])
+            if s == 25:
+                jobs.extend([("X", 1, 0, g, j, "acc%d" % j) for g in range(2) for j in range(4)])
+            if s >= 26 and s % 2 == 0 and s <= 32:
+                jobs.extend([("X", 1, 0, (s - 22) // 2, j, "acc%d" % j) for j in range(4)])
+            if s == 32:
+                jobs.extend([("X", 1, 1, g, j, LATE[j]) for g in range(6) for j in range(4)])
+            if s == 33:
+                jobs.extend([("X", 1, h, 6, j, LATE[j]) for h in range(2) for j in range(4)])
+            if s == 34:
+                jobs.extend([("X", 1, 0, 7, j, LATE[j]) for j in range(4)])
+            if s == 35:
+                jobs.extend([("X", 1, 1, 7, j, LATE[j]) for j in range(4)])
+            return jobs
+
+        def run_job(job):
+            if job[0] == "T":
+                mv_transposes(job[1], job[2])
+            else:
+                mx(job[1], job[2], job[3], job[4], job[5])
+
+        stores["due"] = []
+        load_qk(0)
+        load_mk(0, 0)
+        load_mv(0)
+        load_mk(0, 1)
+        load_qv(0)
+        load_qv(1)
+        load_mv(1)
+        load_mk(0, 2)
+        load_mk(0, 3)
+        for c in range(RING):
+            aff(c)
+
+        for s in range(STEPS + 5):
+            if s % 4 == 0 and 2 <= s // 4 + 1 < 8 and s >= 4:
+                load_mv(s // 4 + 1)
+            if s == 6:
+                load_qk(1)
+            if s in (7, 8, 9, 10):
+                load_mk(1, s - 7)
+            if s in (1, 2, 3):
+                load_qv(s + 1)
+            if s in (28, 29, 30):
+                load_qv(s - 23)
+
+            jobs = pe_extras(s)
+            if s < STEPS:
+                per = (len(jobs) + 1) // 3
+                slots = [jobs[0:1]] + [jobs[1 + i * per : 1 + (i + 1) * per] for i in range(3)]
+                for k in range(4):
+                    c = 4 * s + k
+                    shift_out(c)
+                    if c + RING < NAFF:
+                        aff(c + RING)
+                    for job in slots[k]:
+                        run_job(job)
+            else:
+                for job in jobs:
+                    run_job(job)
+
+            for rho in range(ROUNDS):
+                n_s = len(split_of(rho)["S"])
+                if s == 2 * rho + 3:
+                    for i in range(n_s):
+                        stage(rho, i, [0, 1] if rho < ROUNDS - 2 else [0, 1, 2, 3])
+                if s == 2 * rho + 4 and rho < ROUNDS - 2:
+                    for i in range(n_s):
+                        stage(rho, i, [2, 3])
+            if s < STEPS:
+                exp_tile(s // 2, 2 * (s % 2))
+                exp_tile(s // 2, 2 * (s % 2) + 1)
+                mv_copy(s // 2, s % 2)
+
+            if s % 2 == 0:
+                rho = (s - 4) // 2
+                if 0 <= rho < ROUNDS - 1:
+                    for i in range(len(split_of(rho)["S"])):
+                        regroup(rho, i)
+                rho = (s - 2) // 2
+                if 0 <= rho < ROUNDS:
+                    quantise_mv(rho)
+                if s == STEPS:
+                    quantise_attn(ROUNDS - 2, 0, Q)
+                if 0 <= rho < ROUNDS:
+                    recip(rho)
+                    if rho == ROUNDS - 1:
+                        for q0, q1 in split_of(rho)["V"]:
+                            direct(nc.vector, rho, q0, q1, recs[rho])
+                    q0, q1 = split_of(rho)["G"][0]
+                    direct(nc.gpsimd, rho, q0, q1, recs[rho])
+            else:
+                rho = (s - 5) // 2
+                if 0 <= rho < ROUNDS - 2:
+                    quantise_attn(rho, 0, Q)
+                rho = (s - 3) // 2
+                if 0 <= rho < ROUNDS - 1:
+                    for q0, q1 in split_of(rho)["V"]:
+                        direct(nc.vector, rho, q0, q1, recs[rho])
+                    second_piece(rho)
+            if s == STEPS + 1:
+                regroup(ROUNDS - 1, 0)
+                quantise_attn(ROUNDS - 1, 0, 512)
+                regroup(ROUNDS - 1, 1)
+                quantise_attn(ROUNDS - 1, 512, 1024)
+
+            if s == 20:
+                for j in range(4):
+                    leave("S" if j % 2 == 0 else "V", 0, 0, j)
+            if 21 <= s < 25:
+                leave("S" if s % 2 == 0 else "V", 0, 1, s - 21)
+            if s == 34:
+                for j in range(4):
+                    leave("S" if j % 2 == 0 else "V", 1, 0, j)
+            if s == 35:
+                for j in range(4):
+                    leave("S" if j % 2 == 0 else "V", 1, 1, j)
+
+            flush_stores()
+            if s == 0:
+                cast_qv(0)
+                cast_qv(1)
+            if s in (1, 2, 3):
+                cast_qv(s + 1)
+            if s in (33, 34, 35):
+                cast_qv(s - 28)
+        flush_stores()

@@ -19,25 +19,19 @@ M = 4096
 HALF = 512
 PASSES = 8
 ROUNDS = NS * PASSES
-STEPS = 2 * ROUNDS
-NAFF = 4 * STEPS
+BANKS = 8
+NAFF = BANKS * ROUNDS
 RING = 3
 SCALE = 128.0 ** -0.5
 FLOPS = 2 * NS * Q * M * (128 + CV)
 
-MANUAL = True
-GQ = 224
+GQ = 448
 VQ = 64
-HEAD_CASTS = 5
+SQ = Q - GQ - VQ
 SLOTS = 11
-
-
-def split_of(rho):
-    if rho == ROUNDS - 1:
-        return {"G": [(512, 800)], "S": [(384, 512), (800, 1024)], "V": [(0, 384)]}
-    if rho == ROUNDS - 2:
-        return {"G": [(0, GQ), (GQ, 2 * GQ)], "S": [(2 * GQ + VQ, 1024)], "V": [(2 * GQ, 2 * GQ + VQ)]}
-    return {"G": [(0, GQ), (GQ, 2 * GQ)], "S": [(2 * GQ + VQ, 1024)], "V": [(2 * GQ, 2 * GQ + VQ)]}
+EZ = 2
+LAST = ROUNDS - 1
+SREG = 256
 
 
 def tile_stm_head_kernel(tc, q_key, q_val, m_key, m_val, out):
@@ -55,8 +49,7 @@ def tile_stm_head_kernel(tc, q_key, q_val, m_key, m_val, out):
         keep = ctx.enter_context(tc.tile_pool(name="keep", bufs=SLOTS))
         small = ctx.enter_context(tc.tile_pool(name="small", bufs=4))
         psum = ctx.enter_context(tc.psum_pool(name="psum", bufs=1))
-        if MANUAL:
-            ctx.enter_context(tc.manual_schedule())
+        ctx.enter_context(tc.manual_schedule())
 
         ident = const.tile([P, P], F32)
         make_identity(nc, ident[:])
@@ -80,8 +73,7 @@ def tile_stm_head_kernel(tc, q_key, q_val, m_key, m_val, out):
         tps = {}
         acc = {}
         qv_b = {}
-        qv_f = {}
-        stores = {}
+        stores = {"due": []}
 
         def load_qk(n):
             t = const.tile([P, Q], BF16, name="qk%d" % n)
@@ -101,15 +93,15 @@ def tile_stm_head_kernel(tc, q_key, q_val, m_key, m_val, out):
             mvraw[chunk] = mv_raw
 
         def load_qv(k):
-            qvb = raws.tile([P, Q], BF16, tag="qvb", bufs=3)
+            qvb = raws.tile([P, Q], BF16, tag="qvb", bufs=7)
             nc.sync.dma_start(out=qvb[:], in_=qv_src[k // 4][:, k % 4, :])
             qv_b[k] = qvb
 
         def aff(c):
-            s, k = divmod(c, 4)
-            r, w = divmod(s, 2)
+            r, k = divmod(c, BANKS)
             n, g = divmod(r, PASSES)
-            e, h = k % 2, k // 2
+            w, kk = divmod(k, 4)
+            e, h = kk % 2, kk // 2
             base = 512 * (g % 2) + 256 * w
             ps = psum.tile([P, HALF], F32, tag="ring%d" % (c % RING))
             nc.tensor.matmul(
@@ -122,12 +114,12 @@ def tile_stm_head_kernel(tc, q_key, q_val, m_key, m_val, out):
             ring[c] = ps
 
         def shift_out(c):
-            s, k = divmod(c, 4)
-            r, w = divmod(s, 2)
-            e, h = k % 2, k // 2
+            r, k = divmod(c, BANKS)
+            w, kk = divmod(k, 4)
+            e, h = kk % 2, kk // 2
             t = 2 * w + e
             if r not in e_t:
-                ez = work.tile([P, 4, Q], F32, tag="ez", bufs=3)
+                ez = work.tile([P, 4, Q], F32, tag="ez", bufs=EZ)
                 e_t[r] = ez
             dst = e_t[r][:, t, HALF * h : HALF * h + HALF]
             if h == 0:
@@ -166,42 +158,33 @@ def tile_stm_head_kernel(tc, q_key, q_val, m_key, m_val, out):
             rc = small.tile([P, 4], F32, tag="rc")
             nc.vector.reciprocal(out=rc[:], in_=sums[r][:])
             recs[r] = rc
-            gr = work.tile([P, Q, 4], BF16, tag="gr", align_bytes=64)
-            grouped[r] = gr
 
-        def direct(eng, r, q0, q1, rc):
+        def direct(eng, r, q0, q1):
+            if r not in grouped:
+                gr = work.tile([P, Q, 4], BF16, tag="gr", bufs=1, align_bytes=64)
+                grouped[r] = gr
             eng.tensor_tensor(
                 out=grouped[r][:, q0:q1, :],
                 in0=e_t[r][:, :, q0:q1].rearrange("p t q -> p q t"),
-                in1=rc[:].unsqueeze(1).to_broadcast([P, q1 - q0, 4]),
+                in1=recs[r][:].unsqueeze(1).to_broadcast([P, q1 - q0, 4]),
                 op=ALU.mult,
             )
 
-        def second_piece(r):
-            rc2 = small.tile([P, 4], F32, tag="rc2")
-            nc.vector.tensor_copy(out=rc2[:], in_=recs[r][:])
-            q0, q1 = split_of(r)["G"][1]
-            direct(nc.gpsimd, r, q0, q1, rc2)
-
-        def stage(r, i, ts):
-            q0, q1 = split_of(r)["S"][i]
-            if (r, i) not in staged:
-                ab = work.tile([P, 4, 512], BF16, tag="ab")
-                staged[(r, i)] = ab
-            for t in ts:
+        def stage(r, q0, q1):
+            ab = work.tile([P, 4, 512], BF16, tag="ab")
+            staged[r] = ab
+            for t in range(4):
                 nc.scalar.activation(
-                    out=staged[(r, i)][:, t, 0 : q1 - q0],
-                    in_=e_t[r][:, t, q0:q1],
-                    func=ACT.Copy,
-                    scale=recs[r][:, t : t + 1],
+                    out=ab[:, t, 0 : q1 - q0], in_=e_t[r][:, t, q0:q1], func=ACT.Copy, scale=recs[r][:, t : t + 1]
                 )
 
-        def regroup(r, i):
-            q0, q1 = split_of(r)["S"][i]
-            nc.vector.tensor_copy(
-                out=grouped[r][:, q0:q1, :].rearrange("p (c i) t -> p c t i", i=4),
-                in_=staged[(r, i)][:, :, 0 : q1 - q0].rearrange("p t (c i) -> p c t i", i=4),
-            )
+        def regroup(eng_name, r, base, q0, q1):
+            dst = grouped[r][:, q0:q1, :].rearrange("p (c i) t -> p c t i", i=4)
+            src = staged[r][:, :, q0 - base : q1 - base].rearrange("p t (c i) -> p c t i", i=4)
+            if eng_name == "V":
+                nc.vector.tensor_copy(out=dst, in_=src)
+            else:
+                nc.scalar.copy(out=dst, in_=src)
 
         def quantise_attn(r, q0, q1):
             if r not in a_codes:
@@ -261,9 +244,14 @@ def tile_stm_head_kernel(tc, q_key, q_val, m_key, m_val, out):
                 nc.vector.tensor_copy(out=ost[:], in_=acc[(n, h, j)][:])
             stores["due"].append((out_v[n][:, 4 + j, HALF * h : HALF * h + HALF], ost))
 
-        def cast_qv(k):
-            qvf = raws.tile([P, Q], F32, tag="qvf")
-            nc.gpsimd.tensor_scalar(out=qvf[:], in0=qv_b[k][:], scalar1=1.0, scalar2=0.0, op0=ALU.mult, op1=ALU.add)
+        def cast_qv(eng_name, k):
+            qvf = raws.tile([P, Q], F32, tag="qvf", bufs=7)
+            if eng_name == "G":
+                nc.gpsimd.tensor_scalar(out=qvf[:], in0=qv_b[k][:], scalar1=1.0, scalar2=0.0, op0=ALU.mult, op1=ALU.add)
+            elif eng_name == "V":
+                nc.vector.tensor_copy(out=qvf[:], in_=qv_b[k][:])
+            else:
+                nc.scalar.copy(out=qvf[:], in_=qv_b[k][:])
             stores["due"].append((out_v[k // 4][:, k % 4, :], qvf))
 
         def flush_stores():
@@ -271,139 +259,125 @@ def tile_stm_head_kernel(tc, q_key, q_val, m_key, m_val, out):
                 nc.sync.dma_start(out=dst, in_=src[:])
             stores["due"] = []
 
-        LATE = ["ring0", "ring1", "ring2", "tp"]
-
-        def pe_extras(s):
+        def mx_plan(w):
             jobs = []
-            if s < STEPS:
-                jobs.append(("T", s // 2, s % 2))
-            if s >= 6 and s % 2 == 0 and (s - 6) // 2 < PASSES:
-                jobs.extend([("X", 0, 0, (s - 6) // 2, j, "acc%d" % j) for j in range(4)])
-            if 21 <= s < 25:
-                jobs.extend([("X", 0, 1, g, s - 21, "acc%d" % (s - 21)) for g in range(PASSES)])
-            if s == 25:
-                jobs.extend([("X", 1, 0, g, j, "acc%d" % j) for g in range(2) for j in range(4)])
-            if s >= 26 and s % 2 == 0 and s <= 32:
-                jobs.extend([("X", 1, 0, (s - 22) // 2, j, "acc%d" % j) for j in range(4)])
-            if s == 32:
-                jobs.extend([("X", 1, 1, g, j, LATE[j]) for g in range(6) for j in range(4)])
-            if s == 33:
-                jobs.extend([("X", 1, h, 6, j, LATE[j]) for h in range(2) for j in range(4)])
-            if s == 34:
-                jobs.extend([("X", 1, 0, 7, j, LATE[j]) for j in range(4)])
-            if s == 35:
-                jobs.extend([("X", 1, 1, 7, j, LATE[j]) for j in range(4)])
-            return jobs
-
-        def run_job(job):
-            if job[0] == "T":
-                mv_transposes(job[1], job[2])
+            if 2 <= w < 2 + PASSES:
+                jobs.extend([(0, 0, w - 2, j, "acc%d" % j) for j in range(4)])
+            if w in (10, 11):
+                jobs.extend([(0, 1, g, j, "acc%d" % j) for j in (2 * (w - 10), 2 * (w - 10) + 1) for g in range(PASSES)])
+            if w == 12:
+                jobs.extend([(1, 0, g, j, "acc%d" % j) for g in range(3) for j in range(4)])
+            if 13 <= w < ROUNDS:
+                jobs.extend([(1, 0, w - 10, j, "acc%d" % j) for j in range(4)])
+            plan = dict((k, []) for k in range(BANKS + 1))
+            if w < LAST:
+                for k in range(1, 7):
+                    plan[k] = jobs[k - 1 : k]
+                plan[BANKS] = jobs[6:]
             else:
-                mx(job[1], job[2], job[3], job[4], job[5])
+                jobs.extend([(1, 1, g, 0, "tp") for g in range(6)])
+                for k in range(1, 6):
+                    plan[k] = jobs[2 * k - 2 : 2 * k]
+                for k, j, tag in ((5, 1, "ring2"), (6, 2, "ring0"), (7, 3, "ring1")):
+                    plan[k] = plan[k] + [(1, 1, g, j, tag) for g in range(6)]
+            return plan
 
-        stores["due"] = []
+        def mv_events(r):
+            if r == 0:
+                return {2: (0, 0), 4: (0, 1), 6: (1, 0), 7: (1, 1)}
+            if r < LAST:
+                return {0: (r + 1, 0), 7: (r + 1, 1)}
+            return {}
+
         load_qk(0)
         load_mk(0, 0)
         load_mv(0)
-        load_mk(0, 1)
-        load_qv(0)
-        load_qv(1)
+        for k in range(7):
+            load_qv(k)
         load_mv(1)
-        load_mk(0, 2)
-        load_mk(0, 3)
+        load_mk(0, 1)
         for c in range(RING):
             aff(c)
+        for k in range(3):
+            cast_qv("G", k)
 
-        for s in range(STEPS + 5):
-            if s % 4 == 0 and 2 <= s // 4 + 1 < 8 and s >= 4:
-                load_mv(s // 4 + 1)
-            if s == 6:
+        for r in range(ROUNDS):
+            if r == 0:
+                load_mk(0, 2)
+                load_mk(0, 3)
+            if r % 2 == 1 and 2 <= (r + 3) // 2 < 8:
+                load_mv((r + 3) // 2)
+            if r == 3:
                 load_qk(1)
-            if s in (7, 8, 9, 10):
-                load_mk(1, s - 7)
-            if s in (1, 2, 3):
-                load_qv(s + 1)
-            if s in (28, 29, 30):
-                load_qv(s - 23)
+            if r in (3, 4, 5, 6):
+                load_mk(1, r - 3)
+            if r == 10:
+                load_qv(7)
 
-            jobs = pe_extras(s)
-            if s < STEPS:
-                per = (len(jobs) + 1) // 3
-                slots = [jobs[0:1]] + [jobs[1 + i * per : 1 + (i + 1) * per] for i in range(3)]
-                for k in range(4):
-                    c = 4 * s + k
-                    shift_out(c)
-                    if c + RING < NAFF:
-                        aff(c + RING)
-                    for job in slots[k]:
-                        run_job(job)
-            else:
-                for job in jobs:
-                    run_job(job)
+            plan = mx_plan(r)
+            events = mv_events(r)
+            for k in range(BANKS):
+                c = BANKS * r + k
+                shift_out(c)
+                if c + RING < NAFF:
+                    aff(c + RING)
+                if k in events:
+                    mv_transposes(*events[k])
+                for job in plan[k]:
+                    mx(*job)
+                if k % 4 >= 2:
+                    exp_tile(r, 2 * (k // 4) + k % 2)
+                if k in events:
+                    mv_copy(*events[k])
+            for job in plan[BANKS]:
+                mx(*job)
 
-            for rho in range(ROUNDS):
-                n_s = len(split_of(rho)["S"])
-                if s == 2 * rho + 3:
-                    for i in range(n_s):
-                        stage(rho, i, [0, 1] if rho < ROUNDS - 2 else [0, 1, 2, 3])
-                if s == 2 * rho + 4 and rho < ROUNDS - 2:
-                    for i in range(n_s):
-                        stage(rho, i, [2, 3])
-            if s < STEPS:
-                exp_tile(s // 2, 2 * (s % 2))
-                exp_tile(s // 2, 2 * (s % 2) + 1)
-                mv_copy(s // 2, s % 2)
+            if r == 9:
+                leave("V", 0, 0, 0)
+                leave("V", 0, 0, 1)
 
-            if s % 2 == 0:
-                rho = (s - 4) // 2
-                if 0 <= rho < ROUNDS - 1:
-                    for i in range(len(split_of(rho)["S"])):
-                        regroup(rho, i)
-                rho = (s - 2) // 2
-                if 0 <= rho < ROUNDS:
-                    quantise_mv(rho)
-                if s == STEPS:
-                    quantise_attn(ROUNDS - 2, 0, Q)
-                if 0 <= rho < ROUNDS:
-                    recip(rho)
-                    if rho == ROUNDS - 1:
-                        for q0, q1 in split_of(rho)["V"]:
-                            direct(nc.vector, rho, q0, q1, recs[rho])
-                    q0, q1 = split_of(rho)["G"][0]
-                    direct(nc.gpsimd, rho, q0, q1, recs[rho])
-            else:
-                rho = (s - 5) // 2
-                if 0 <= rho < ROUNDS - 2:
-                    quantise_attn(rho, 0, Q)
-                rho = (s - 3) // 2
-                if 0 <= rho < ROUNDS - 1:
-                    for q0, q1 in split_of(rho)["V"]:
-                        direct(nc.vector, rho, q0, q1, recs[rho])
-                    second_piece(rho)
-            if s == STEPS + 1:
-                regroup(ROUNDS - 1, 0)
-                quantise_attn(ROUNDS - 1, 0, 512)
-                regroup(ROUNDS - 1, 1)
-                quantise_attn(ROUNDS - 1, 512, 1024)
+            if r == 0:
+                for k in range(3, 7):
+                    cast_qv("V", k)
+            if r >= 1:
+                direct(nc.vector, r - 1, GQ, GQ + VQ)
+                regroup("V", r - 1, GQ + VQ, GQ + VQ, Q)
+            quantise_mv(r)
+            if r in (10, 11):
+                leave("V", 0, 1, 2 * (r - 10))
+            recip(r)
+            if r >= 1:
+                quantise_attn(r - 1, 0, Q)
 
-            if s == 20:
-                for j in range(4):
-                    leave("S" if j % 2 == 0 else "V", 0, 0, j)
-            if 21 <= s < 25:
-                leave("S" if s % 2 == 0 else "V", 0, 1, s - 21)
-            if s == 34:
-                for j in range(4):
-                    leave("S" if j % 2 == 0 else "V", 1, 0, j)
-            if s == 35:
-                for j in range(4):
-                    leave("S" if j % 2 == 0 else "V", 1, 1, j)
-
+            if r < LAST:
+                direct(nc.gpsimd, r, 0, GQ)
+            if r == 9:
+                leave("S", 0, 0, 2)
+                leave("S", 0, 0, 3)
+            if r < LAST:
+                stage(r, GQ + VQ, Q)
+            if r in (10, 11):
+                leave("S", 0, 1, 2 * (r - 10) + 1)
             flush_stores()
-            if s == 0:
-                cast_qv(0)
-                cast_qv(1)
-            if s in (1, 2, 3):
-                cast_qv(s + 1)
-            if s in (33, 34, 35):
-                cast_qv(s - 28)
+
+        cast_qv("S", 7)
+        stage(LAST, HALF, Q)
+        for h in range(2):
+            for j in range(4):
+                mx(1, h, 6, j, "")
+        direct(nc.vector, LAST, 0, HALF)
+        regroup("S", LAST, HALF, Q - SREG, Q)
+        flush_stores()
+        quantise_attn(LAST, 0, HALF)
+        regroup("V", LAST, HALF, HALF, Q - SREG)
+        quantise_attn(LAST, HALF, Q)
+        for j in range(4):
+            mx(1, 0, 7, j, "")
+        for j in range(4):
+            leave("S", 1, 0, j)
+        flush_stores()
+        for j in range(4):
+            mx(1, 1, 7, j, "")
+        for j in range(4):
+            leave("V" if j % 2 == 0 else "S", 1, 1, j)
         flush_stores()

@@ -25,7 +25,7 @@ RING = 3
 SCALE = 128.0 ** -0.5
 FLOPS = 2 * NS * Q * M * (128 + CV)
 
-GQ = 448
+GQ = 512
 VQ = 64
 SQ = Q - GQ - VQ
 SLOTS = 11
@@ -75,15 +75,16 @@ def tile_stm_head_kernel(tc, q_key, q_val, m_key, m_val, out):
         qv_b = {}
         stores = {"due": []}
 
-        def load_qk(n):
-            t = const.tile([P, Q], BF16, name="qk%d" % n)
-            nc.sync.dma_start(out=t[:], in_=qk_src[n])
-            qk[n] = t
+        def load_qk(n, h):
+            t = const.tile([P, HALF], BF16, name="qk%d_%d" % (n, h))
+            nc.sync.dma_start(out=t[:], in_=qk_src[n][:, HALF * h : HALF * h + HALF])
+            qk[(n, h)] = t
 
-        def load_mk(n, quarter):
-            t = const.tile([P, 1024], BF16, name="mk%d_%d" % (n, quarter))
-            nc.sync.dma_start(out=t[:], in_=mk_src[n][:, 1024 * quarter : 1024 * quarter + 1024])
-            mk[(n, quarter)] = t
+        def load_mk(n, g0, g1):
+            t = const.tile([P, 512 * (g1 - g0)], BF16, name="mk%d_%d" % (n, g0))
+            nc.sync.dma_start(out=t[:], in_=mk_src[n][:, 512 * g0 : 512 * g1])
+            for g in range(g0, g1):
+                mk[(n, g)] = t[:, 512 * (g - g0) : 512 * (g - g0) + 512]
 
         def load_mv(chunk):
             n = chunk // 4
@@ -102,12 +103,11 @@ def tile_stm_head_kernel(tc, q_key, q_val, m_key, m_val, out):
             n, g = divmod(r, PASSES)
             w, kk = divmod(k, 4)
             e, h = kk % 2, kk // 2
-            base = 512 * (g % 2) + 256 * w
             ps = psum.tile([P, HALF], F32, tag="ring%d" % (c % RING))
             nc.tensor.matmul(
                 out=ps[:],
-                lhsT=mk[(n, g // 2)][:, base + e : base + 256 : 2],
-                rhs=qk[n][:, HALF * h : HALF * h + HALF],
+                lhsT=mk[(n, g)][:, 256 * w + e : 256 * w + 256 : 2],
+                rhs=qk[(n, h)][:],
                 start=True,
                 stop=True,
             )
@@ -209,7 +209,7 @@ def tile_stm_head_kernel(tc, q_key, q_val, m_key, m_val, out):
 
         def mv_copy(r, b):
             if r not in gmv:
-                gm = work.tile([P, 4 * CV], BF16, tag="gmv", align_bytes=64)
+                gm = work.tile([P, 4 * CV], BF16, tag="gmv", bufs=3, align_bytes=64)
                 gmv[r] = gm
             words = gmv[r][:].bitcast(F32).rearrange("p (j c u) -> p j c u", j=4, u=2)
             nc.scalar.copy(out=words[:, 2 * b : 2 * b + 2], in_=tps[(r, b)][:].rearrange("p j u c -> p j c u"))
@@ -237,12 +237,19 @@ def tile_stm_head_kernel(tc, q_key, q_val, m_key, m_val, out):
             )
 
         def leave(eng_name, n, h, j):
-            ost = work.tile([P, HALF], F32, tag="ost", bufs=4)
-            if eng_name == "S":
-                nc.scalar.copy(out=ost[:], in_=acc[(n, h, j)][:])
+            if n == 0:
+                ost = work.tile([P, HALF], F32, tag="ost", bufs=4)
+                dst = ost[:]
             else:
-                nc.vector.tensor_copy(out=ost[:], in_=acc[(n, h, j)][:])
-            stores["due"].append((out_v[n][:, 4 + j, HALF * h : HALF * h + HALF], ost))
+                if (h, "end") not in acc:
+                    big = raws.tile([P, 4, HALF], F32, tag="mvraw")
+                    acc[(h, "end")] = big
+                dst = acc[(h, "end")][:, j, :]
+            if eng_name == "S":
+                nc.scalar.copy(out=dst, in_=acc[(n, h, j)][:])
+            else:
+                nc.vector.tensor_copy(out=dst, in_=acc[(n, h, j)][:])
+            stores["due"].append((out_v[n][:, 4 + j, HALF * h : HALF * h + HALF], dst))
 
         def cast_qv(eng_name, k):
             qvf = raws.tile([P, Q], F32, tag="qvf", bufs=7)
@@ -252,11 +259,11 @@ def tile_stm_head_kernel(tc, q_key, q_val, m_key, m_val, out):
                 nc.vector.tensor_copy(out=qvf[:], in_=qv_b[k][:])
             else:
                 nc.scalar.copy(out=qvf[:], in_=qv_b[k][:])
-            stores["due"].append((out_v[k // 4][:, k % 4, :], qvf))
+            stores["due"].append((out_v[k // 4][:, k % 4, :], qvf[:]))
 
         def flush_stores():
             for dst, src in stores["due"]:
-                nc.sync.dma_start(out=dst, in_=src[:])
+                nc.sync.dma_start(out=dst, in_=src)
             stores["due"] = []
 
         def mx_plan(w):
@@ -276,41 +283,49 @@ def tile_stm_head_kernel(tc, q_key, q_val, m_key, m_val, out):
                 plan[BANKS] = jobs[6:]
             else:
                 jobs.extend([(1, 1, g, 0, "tp") for g in range(6)])
-                for k in range(1, 6):
-                    plan[k] = jobs[2 * k - 2 : 2 * k]
+                for k in range(5):
+                    plan[k] = jobs[2 * k : 2 * k + 2]
                 for k, j, tag in ((5, 1, "ring2"), (6, 2, "ring0"), (7, 3, "ring1")):
-                    plan[k] = plan[k] + [(1, 1, g, j, tag) for g in range(6)]
+                    plan[k] = [(1, 1, g, j, tag) for g in range(6)]
             return plan
 
         def mv_events(r):
             if r == 0:
-                return {2: (0, 0), 4: (0, 1), 6: (1, 0), 7: (1, 1)}
-            if r < LAST:
-                return {0: (r + 1, 0), 7: (r + 1, 1)}
+                return {4: (0, 0), 7: (0, 1), 8: (1, 0)}
+            if r < LAST - 1:
+                return {0: (r, 1), 7: (r + 1, 0)}
+            if r == LAST - 1:
+                return {0: (r, 1), 4: (LAST, 0), 7: (LAST, 1)}
             return {}
 
-        load_qk(0)
-        load_mk(0, 0)
+        load_qk(0, 0)
+        load_mk(0, 0, 1)
+        load_qk(0, 1)
+        for k in range(3):
+            load_qv(k)
         load_mv(0)
-        for k in range(7):
+        load_mk(0, 1, 2)
+        for k in range(3, 7):
             load_qv(k)
         load_mv(1)
-        load_mk(0, 1)
+        load_mk(0, 2, 4)
         for c in range(RING):
             aff(c)
-        for k in range(3):
-            cast_qv("G", k)
+        cast_qv("S", 0)
+        cast_qv("G", 1)
+        cast_qv("G", 2)
 
         for r in range(ROUNDS):
             if r == 0:
-                load_mk(0, 2)
-                load_mk(0, 3)
-            if r % 2 == 1 and 2 <= (r + 3) // 2 < 8:
-                load_mv((r + 3) // 2)
+                load_mk(0, 4, 6)
+                load_mk(0, 6, 8)
+            if r % 2 == 0 and 2 <= (r + 2) // 2 < 8:
+                load_mv((r + 2) // 2)
             if r == 3:
-                load_qk(1)
+                load_qk(1, 0)
+                load_qk(1, 1)
             if r in (3, 4, 5, 6):
-                load_mk(1, r - 3)
+                load_mk(1, 2 * (r - 3), 2 * (r - 3) + 2)
             if r == 10:
                 load_qv(7)
 
@@ -329,6 +344,9 @@ def tile_stm_head_kernel(tc, q_key, q_val, m_key, m_val, out):
                     exp_tile(r, 2 * (k // 4) + k % 2)
                 if k in events:
                     mv_copy(*events[k])
+            if BANKS in events:
+                mv_transposes(*events[BANKS])
+                mv_copy(*events[BANKS])
             for job in plan[BANKS]:
                 mx(*job)
 
@@ -342,7 +360,10 @@ def tile_stm_head_kernel(tc, q_key, q_val, m_key, m_val, out):
             if r >= 1:
                 direct(nc.vector, r - 1, GQ, GQ + VQ)
                 regroup("V", r - 1, GQ + VQ, GQ + VQ, Q)
-            quantise_mv(r)
+            if r == 1:
+                quantise_mv(0)
+            if r >= 1:
+                quantise_mv(r)
             if r in (10, 11):
                 leave("V", 0, 1, 2 * (r - 10))
             recip(r)

@@ -154,10 +154,11 @@ def tile_stm_head_kernel(tc, q_key, q_val, m_key, m_val, out):
                 accum_out=sums[r][:, t : t + 1],
             )
 
-        def recip(r):
-            rc = small.tile([P, 4], F32, tag="rc")
-            nc.vector.reciprocal(out=rc[:], in_=sums[r][:])
-            recs[r] = rc
+        def recip(r, pair):
+            if r not in recs:
+                rc = small.tile([P, 4], F32, tag="rc")
+                recs[r] = rc
+            nc.vector.reciprocal(out=recs[r][:, 2 * pair : 2 * pair + 2], in_=sums[r][:, 2 * pair : 2 * pair + 2])
 
         def direct(eng, r, q0, q1):
             if r not in grouped:
@@ -360,15 +361,19 @@ def tile_stm_head_kernel(tc, q_key, q_val, m_key, m_val, out):
             if r >= 1:
                 direct(nc.vector, r - 1, GQ, GQ + VQ)
                 regroup("V", r - 1, GQ + VQ, GQ + VQ, Q)
+            recip(r, 0)
             if r == 1:
                 quantise_mv(0)
             if r >= 1:
                 quantise_mv(r)
             if r in (10, 11):
                 leave("V", 0, 1, 2 * (r - 10))
-            recip(r)
+            if r == LAST:
+                recip(r, 1)
             if r >= 1:
                 quantise_attn(r - 1, 0, Q)
+            if r < LAST:
+                recip(r, 1)
 
             if r < LAST:
                 direct(nc.gpsimd, r, 0, GQ)

@@ -25,7 +25,7 @@ RING = 3
 SCALE = 128.0 ** -0.5
 FLOPS = 2 * NS * Q * M * (128 + CV)
 
-GQ = 512
+GQ = 480
 VQ = 64
 SQ = Q - GQ - VQ
 SLOTS = 11
@@ -201,7 +201,7 @@ def tile_stm_head_kernel(tc, q_key, q_val, m_key, m_val, out):
 
         def mv_transposes(r, b):
             rawf = mvraw[r // 2][:].bitcast(F32)
-            tp = psum.tile([P, 2, 2, P], F32, tag="tp")
+            tp = psum.tile([P, 2, 2, P], F32, tag=("acc%d" % (2 * r + b) if r < 2 else "tp"))
             for jj in range(2):
                 for u in range(2):
                     w0 = 256 * (r % 2) + 128 * u
@@ -279,9 +279,10 @@ def tile_stm_head_kernel(tc, q_key, q_val, m_key, m_val, out):
                 jobs.extend([(1, 0, w - 10, j, "acc%d" % j) for j in range(4)])
             plan = dict((k, []) for k in range(BANKS + 1))
             if w < LAST:
+                early = max(0, len(jobs) - 10)
                 for k in range(1, 7):
-                    plan[k] = jobs[k - 1 : k]
-                plan[BANKS] = jobs[6:]
+                    plan[k] = jobs[:early][k - 1 : k]
+                plan[BANKS] = jobs[early:]
             else:
                 jobs.extend([(1, 1, g, 0, "tp") for g in range(6)])
                 for k in range(5):
@@ -291,12 +292,8 @@ def tile_stm_head_kernel(tc, q_key, q_val, m_key, m_val, out):
             return plan
 
         def mv_events(r):
-            if r == 0:
-                return {4: (0, 0), 7: (0, 1), 8: (1, 0)}
-            if r < LAST - 1:
-                return {0: (r, 1), 7: (r + 1, 0)}
-            if r == LAST - 1:
-                return {0: (r, 1), 4: (LAST, 0), 7: (LAST, 1)}
+            if r < LAST:
+                return {7: (r + 1, 0), 9: (r + 1, 1)}
             return {}
 
         load_qk(0, 0)
@@ -306,28 +303,28 @@ def tile_stm_head_kernel(tc, q_key, q_val, m_key, m_val, out):
             load_qv(k)
         load_mv(0)
         load_mk(0, 1, 2)
-        for k in range(3, 7):
+        for k in range(3, 6):
             load_qv(k)
         load_mv(1)
         load_mk(0, 2, 4)
         for c in range(RING):
             aff(c)
-        cast_qv("S", 0)
-        cast_qv("G", 1)
-        cast_qv("G", 2)
+        for k in range(3):
+            cast_qv("G", k)
 
         for r in range(ROUNDS):
             if r == 0:
                 load_mk(0, 4, 6)
                 load_mk(0, 6, 8)
-            if r % 2 == 0 and 2 <= (r + 2) // 2 < 8:
-                load_mv((r + 2) // 2)
+            if r % 2 == 1 and 2 <= (r + 3) // 2 < 8:
+                load_mv((r + 3) // 2)
             if r == 3:
                 load_qk(1, 0)
                 load_qk(1, 1)
             if r in (3, 4, 5, 6):
                 load_mk(1, 2 * (r - 3), 2 * (r - 3) + 2)
             if r == 10:
+                load_qv(6)
                 load_qv(7)
 
             plan = mx_plan(r)
@@ -337,26 +334,28 @@ def tile_stm_head_kernel(tc, q_key, q_val, m_key, m_val, out):
                 shift_out(c)
                 if c + RING < NAFF:
                     aff(c + RING)
+                if r == 0 and k == 6:
+                    mv_transposes(0, 0)
+                    mv_transposes(0, 1)
                 if k in events:
                     mv_transposes(*events[k])
                 for job in plan[k]:
                     mx(*job)
                 if k % 4 >= 2:
                     exp_tile(r, 2 * (k // 4) + k % 2)
+                if r == 0 and k == 7:
+                    mv_copy(0, 0)
+                    mv_copy(0, 1)
                 if k in events:
                     mv_copy(*events[k])
-            if BANKS in events:
-                mv_transposes(*events[BANKS])
-                mv_copy(*events[BANKS])
             for job in plan[BANKS]:
                 mx(*job)
+            if 9 in events:
+                mv_transposes(*events[9])
 
-            if r == 9:
-                leave("V", 0, 0, 0)
-                leave("V", 0, 0, 1)
 
             if r == 0:
-                for k in range(3, 7):
+                for k in range(3, 6):
                     cast_qv("V", k)
             if r >= 1:
                 direct(nc.vector, r - 1, GQ, GQ + VQ)
@@ -366,6 +365,9 @@ def tile_stm_head_kernel(tc, q_key, q_val, m_key, m_val, out):
                 quantise_mv(0)
             if r >= 1:
                 quantise_mv(r)
+            if r == 9:
+                leave("V", 0, 0, 0)
+                leave("V", 0, 0, 1)
             if r in (10, 11):
                 leave("V", 0, 1, 2 * (r - 10))
             if r == LAST:
@@ -377,22 +379,25 @@ def tile_stm_head_kernel(tc, q_key, q_val, m_key, m_val, out):
 
             if r < LAST:
                 direct(nc.gpsimd, r, 0, GQ)
+            if r < LAST:
+                stage(r, GQ + VQ, Q)
             if r == 9:
                 leave("S", 0, 0, 2)
                 leave("S", 0, 0, 3)
-            if r < LAST:
-                stage(r, GQ + VQ, Q)
             if r in (10, 11):
                 leave("S", 0, 1, 2 * (r - 10) + 1)
+            if 9 in events:
+                mv_copy(*events[9])
             flush_stores()
 
-        cast_qv("S", 7)
+        cast_qv("S", 6)
         stage(LAST, HALF, Q)
         for h in range(2):
             for j in range(4):
                 mx(1, h, 6, j, "")
         direct(nc.vector, LAST, 0, HALF)
         regroup("S", LAST, HALF, Q - SREG, Q)
+        cast_qv("S", 7)
         flush_stores()
         quantise_attn(LAST, 0, HALF)
         regroup("V", LAST, HALF, HALF, Q - SREG)
@@ -400,7 +405,7 @@ def tile_stm_head_kernel(tc, q_key, q_val, m_key, m_val, out):
         for j in range(4):
             mx(1, 0, 7, j, "")
         for j in range(4):
-            leave("S", 1, 0, j)
+            leave("S" if j < 3 else "V", 1, 0, j)
         flush_stores()
         for j in range(4):
             mx(1, 1, 7, j, "")

@@ -25,8 +25,8 @@ RING = 3
 SCALE = 128.0 ** -0.5
 FLOPS = 2 * NS * Q * M * (128 + CV)
 
-GQ = 480
-VQ = 64
+GQ = 448
+VQ = 72
 SQ = Q - GQ - VQ
 SLOTS = 11
 EZ = 2
@@ -172,7 +172,7 @@ def tile_stm_head_kernel(tc, q_key, q_val, m_key, m_val, out):
             )
 
         def stage(r, q0, q1):
-            ab = work.tile([P, 4, 512], BF16, tag="ab")
+            ab = work.tile([P, 4, max(SQ, HALF)], BF16, tag="ab")
             staged[r] = ab
             for t in range(4):
                 nc.scalar.activation(

@@ -25,8 +25,8 @@ RING = 3
 SCALE = 128.0 ** -0.5
 FLOPS = 2 * NS * Q * M * (128 + CV)
 
-GQ = 448
-VQ = 72
+GQ = 544
+VQ = 40
 SQ = Q - GQ - VQ
 SLOTS = 11
 EZ = 2

@@ -25,13 +25,12 @@ RING = 3
 SCALE = 128.0 ** -0.5
 FLOPS = 2 * NS * Q * M * (128 + CV)
 
-GQ = 544
-VQ = 40
-SQ = Q - GQ - VQ
+GQ = 584
+SQ = Q - GQ
 SLOTS = 11
 EZ = 2
 LAST = ROUNDS - 1
-SREG = 256
+SREG = 320
 
 
 def tile_stm_head_kernel(tc, q_key, q_val, m_key, m_val, out):
@@ -94,7 +93,7 @@ def tile_stm_head_kernel(tc, q_key, q_val, m_key, m_val, out):
             mvraw[chunk] = mv_raw
 
         def load_qv(k):
-            qvb = raws.tile([P, Q], BF16, tag="qvb", bufs=7)
+            qvb = raws.tile([P, Q], BF16, tag="qvb", bufs=6)
             nc.sync.dma_start(out=qvb[:], in_=qv_src[k // 4][:, k % 4, :])
             qv_b[k] = qvb
 
@@ -253,7 +252,7 @@ def tile_stm_head_kernel(tc, q_key, q_val, m_key, m_val, out):
             stores["due"].append((out_v[n][:, 4 + j, HALF * h : HALF * h + HALF], dst))
 
         def cast_qv(eng_name, k):
-            qvf = raws.tile([P, Q], F32, tag="qvf", bufs=7)
+            qvf = raws.tile([P, Q], F32, tag="qvf", bufs=8)
             if eng_name == "G":
                 nc.gpsimd.tensor_scalar(out=qvf[:], in0=qv_b[k][:], scalar1=1.0, scalar2=0.0, op0=ALU.mult, op1=ALU.add)
             elif eng_name == "V":
@@ -301,16 +300,19 @@ def tile_stm_head_kernel(tc, q_key, q_val, m_key, m_val, out):
         load_qk(0, 1)
         for k in range(3):
             load_qv(k)
-        load_mv(0)
         load_mk(0, 1, 2)
-        for k in range(3, 6):
+        for k in range(3, 5):
             load_qv(k)
-        load_mv(1)
+        load_mv(0)
+        load_qv(5)
         load_mk(0, 2, 4)
         for c in range(RING):
             aff(c)
-        for k in range(3):
+        for k in range(5):
             cast_qv("G", k)
+        load_qv(6)
+        load_qv(7)
+        load_mv(1)
 
         for r in range(ROUNDS):
             if r == 0:
@@ -323,9 +325,6 @@ def tile_stm_head_kernel(tc, q_key, q_val, m_key, m_val, out):
                 load_qk(1, 1)
             if r in (3, 4, 5, 6):
                 load_mk(1, 2 * (r - 3), 2 * (r - 3) + 2)
-            if r == 10:
-                load_qv(6)
-                load_qv(7)
 
             plan = mx_plan(r)
             events = mv_events(r)
@@ -355,11 +354,10 @@ def tile_stm_head_kernel(tc, q_key, q_val, m_key, m_val, out):
 
 
             if r == 0:
-                for k in range(3, 6):
+                for k in range(5, 8):
                     cast_qv("V", k)
             if r >= 1:
-                direct(nc.vector, r - 1, GQ, GQ + VQ)
-                regroup("V", r - 1, GQ + VQ, GQ + VQ, Q)
+                regroup("V", r - 1, GQ, GQ, Q)
             recip(r, 0)
             if r == 1:
                 quantise_mv(0)
@@ -370,17 +368,14 @@ def tile_stm_head_kernel(tc, q_key, q_val, m_key, m_val, out):
                 leave("V", 0, 0, 1)
             if r in (10, 11):
                 leave("V", 0, 1, 2 * (r - 10))
-            if r == LAST:
-                recip(r, 1)
             if r >= 1:
                 quantise_attn(r - 1, 0, Q)
-            if r < LAST:
-                recip(r, 1)
+            recip(r, 1)
 
             if r < LAST:
                 direct(nc.gpsimd, r, 0, GQ)
             if r < LAST:
-                stage(r, GQ + VQ, Q)
+                stage(r, GQ, Q)
             if r == 9:
                 leave("S", 0, 0, 2)
                 leave("S", 0, 0, 3)
@@ -390,15 +385,12 @@ def tile_stm_head_kernel(tc, q_key, q_val, m_key, m_val, out):
                 mv_copy(*events[9])
             flush_stores()
 
-        cast_qv("S", 6)
         stage(LAST, HALF, Q)
         for h in range(2):
             for j in range(4):
                 mx(1, h, 6, j, "")
         direct(nc.vector, LAST, 0, HALF)
         regroup("S", LAST, HALF, Q - SREG, Q)
-        cast_qv("S", 7)
-        flush_stores()
         quantise_attn(LAST, 0, HALF)
         regroup("V", LAST, HALF, HALF, Q - SREG)
         quantise_attn(LAST, HALF, Q)

@@ -25,7 +25,7 @@ RING = 3
 SCALE = 128.0 ** -0.5
 FLOPS = 2 * NS * Q * M * (128 + CV)
 
-GQ = 584
+GQ = 544
 SQ = Q - GQ
 SLOTS = 11
 EZ = 2

@@ -27,6 +27,7 @@ FLOPS = 2 * NS * Q * M * (128 + CV)
 
 GQ = 544
 SQ = Q - GQ
+RUN = 2
 SLOTS = 11
 EZ = 2
 LAST = ROUNDS - 1
@@ -164,9 +165,9 @@ def tile_stm_head_kernel(tc, q_key, q_val, m_key, m_val, out):
                 gr = work.tile([P, Q, 4], BF16, tag="gr", bufs=1, align_bytes=64)
                 grouped[r] = gr
             eng.tensor_tensor(
-                out=grouped[r][:, q0:q1, :],
-                in0=e_t[r][:, :, q0:q1].rearrange("p t q -> p q t"),
-                in1=recs[r][:].unsqueeze(1).to_broadcast([P, q1 - q0, 4]),
+                out=grouped[r][:, q0:q1, :].rearrange("p (c i) t -> p c t i", i=RUN),
+                in0=e_t[r][:, :, q0:q1].rearrange("p t (c i) -> p c t i", i=RUN),
+                in1=recs[r][:].unsqueeze(1).unsqueeze(3).to_broadcast([P, (q1 - q0) // RUN, 4, RUN]),
                 op=ALU.mult,
             )
 

from contextlib import ExitStack

import concourse.mybir as mybir
from concourse.masks import make_identity

F32 = mybir.dt.float32
BF16 = mybir.dt.bfloat16
U32 = mybir.dt.uint32
U8 = mybir.dt.uint8
FP8X4 = mybir.dt.float8_e4m3fn_x4
ALU = mybir.AluOpType
ACT = mybir.ActivationFunctionType

P = 128
NS = 2
CV = 512
Q = 1024
M = 4096
HALF = 512
PASSES = 8
ROUNDS = NS * PASSES
BANKS = 8
NAFF = BANKS * ROUNDS
RING = 3
SCALE = 128.0 ** -0.5
FLOPS = 2 * NS * Q * M * (128 + CV)

GQ = 544
SQ = Q - GQ
RUN = 2
SLOTS = 11
EZ = 2
LAST = ROUNDS - 1
SREG = 320


def tile_stm_head_kernel(tc, q_key, q_val, m_key, m_val, out):
    nc = tc.nc
    qk_src = [q_key[n].rearrange("c h w -> c (h w)") for n in range(NS)]
    mk_src = [m_key[n].rearrange("c t h w -> c (t h w)") for n in range(NS)]
    mv_src = [m_val[n].rearrange("(j c) t h w -> c j (t h w)", c=P) for n in range(NS)]
    qv_src = [q_val[n].rearrange("(j c) h w -> c j (h w)", c=P) for n in range(NS)]
    out_v = [out[n].rearrange("(j c) h w -> c j (h w)", c=P) for n in range(NS)]

    with ExitStack() as ctx:
        const = ctx.enter_context(tc.tile_pool(name="const", bufs=1))
        raws = ctx.enter_context(tc.tile_pool(name="raws", bufs=2))
        work = ctx.enter_context(tc.tile_pool(name="work", bufs=2))
        keep = ctx.enter_context(tc.tile_pool(name="keep", bufs=SLOTS))
        small = ctx.enter_context(tc.tile_pool(name="small", bufs=4))
        psum = ctx.enter_context(tc.psum_pool(name="psum", bufs=1))
        ctx.enter_context(tc.manual_schedule())

        ident = const.tile([P, P], F32)
        make_identity(nc, ident[:])

        qk = {}
        mk = {}
        mvraw = {}
        ring = {}
        e_t = {}
        m_first = {}
        m_all = {}
        sums = {}
        recs = {}
        grouped = {}
        staged = {}
        a_codes = {}
        a_scales = {}
        gmv = {}
        v_codes = {}
        v_scales = {}
        tps = {}
        acc = {}
        qv_b = {}
        stores = {"due": []}

        def load_qk(n, h):
            t = const.tile([P, HALF], BF16, name="qk%d_%d" % (n, h))
            nc.sync.dma_start(out=t[:], in_=qk_src[n][:, HALF * h : HALF * h + HALF])
            qk[(n, h)] = t

        def load_mk(n, g0, g1):
            t = const.tile([P, 512 * (g1 - g0)], BF16, name="mk%d_%d" % (n, g0))
            nc.sync.dma_start(out=t[:], in_=mk_src[n][:, 512 * g0 : 512 * g1])
            for g in range(g0, g1):
                mk[(n, g)] = t[:, 512 * (g - g0) : 512 * (g - g0) + 512]

        def load_mv(chunk):
            n = chunk // 4
            col = 1024 * (chunk % 4)
            mv_raw = raws.tile([P, 4, 1024], BF16, tag="mvraw")
            nc.sync.dma_start(out=mv_raw[:], in_=mv_src[n][:, :, col : col + 1024])
            mvraw[chunk] = mv_raw

        def load_qv(k):
            qvb = raws.tile([P, Q], BF16, tag="qvb", bufs=6)
            nc.sync.dma_start(out=qvb[:], in_=qv_src[k // 4][:, k % 4, :])
            qv_b[k] = qvb

        def aff(c):
            r, k = divmod(c, BANKS)
            n, g = divmod(r, PASSES)
            w, kk = divmod(k, 4)
            e, h = kk % 2, kk // 2
            ps = psum.tile([P, HALF], F32, tag="ring%d" % (c % RING))
            nc.tensor.matmul(
                out=ps[:],
                lhsT=mk[(n, g)][:, 256 * w + e : 256 * w + 256 : 2],
                rhs=qk[(n, h)][:],
                start=True,
                stop=True,
            )
            ring[c] = ps

        def shift_out(c):
            r, k = divmod(c, BANKS)
            w, kk = divmod(k, 4)
            e, h = kk % 2, kk // 2
            t = 2 * w + e
            if r not in e_t:
                ez = work.tile([P, 4, Q], F32, tag="ez", bufs=EZ)
                e_t[r] = ez
            dst = e_t[r][:, t, HALF * h : HALF * h + HALF]
            if h == 0:
                mf = small.tile([P, 1], F32, tag="mf")
                m_first[(r, t)] = mf
                nc.vector.tensor_scalar(
                    out=dst, in0=ring[c][:], scalar1=-SCALE, scalar2=None, op0=ALU.mult, op1=ALU.min, accum_out=mf[:]
                )
            else:
                ma = small.tile([P, 1], F32, tag="ma", bufs=8)
                m_all[(r, t)] = ma
                nc.vector.tensor_scalar(
                    out=dst,
                    in0=ring[c][:],
                    scalar1=-SCALE,
                    scalar2=m_first[(r, t)][:],
                    op0=ALU.mult,
                    op1=ALU.min,
                    accum_out=ma[:],
                )

        def exp_tile(r, t):
            if r not in sums:
                sm = small.tile([P, 4], F32, tag="sm")
                sums[r] = sm
            nc.scalar.activation(
                out=e_t[r][:, t, :],
                in_=e_t[r][:, t, :],
                func=ACT.Exp,
                bias=m_all[(r, t)][:],
                scale=-1.0,
                accum_out=sums[r][:, t : t + 1],
            )

        def recip(r, pair):
            if r not in recs:
                rc = small.tile([P, 4], F32, tag="rc")
                recs[r] = rc
            nc.vector.reciprocal(out=recs[r][:, 2 * pair : 2 * pair + 2], in_=sums[r][:, 2 * pair : 2 * pair + 2])

        def direct(eng, r, q0, q1):
            if r not in grouped:
                gr = work.tile([P, Q, 4], BF16, tag="gr", bufs=1, align_bytes=64)
                grouped[r] = gr
            eng.tensor_tensor(
                out=grouped[r][:, q0:q1, :].rearrange("p (c i) t -> p c t i", i=RUN),
                in0=e_t[r][:, :, q0:q1].rearrange("p t (c i) -> p c t i", i=RUN),
                in1=recs[r][:].unsqueeze(1).unsqueeze(3).to_broadcast([P, (q1 - q0) // RUN, 4, RUN]),
                op=ALU.mult,
            )

        def stage(r, q0, q1):
            ab = work.tile([P, 4, max(SQ, HALF)], BF16, tag="ab")
            staged[r] = ab
            for t in range(4):
                nc.scalar.activation(
                    out=ab[:, t, 0 : q1 - q0], in_=e_t[r][:, t, q0:q1], func=ACT.Copy, scale=recs[r][:, t : t + 1]
                )

        def regroup(eng_name, r, base, q0, q1):
            dst = grouped[r][:, q0:q1, :].rearrange("p (c i) t -> p c t i", i=4)
            src = staged[r][:, :, q0 - base : q1 - base].rearrange("p t (c i) -> p c t i", i=4)
            if eng_name == "V":
                nc.vector.tensor_copy(out=dst, in_=src)
            else:
                nc.scalar.copy(out=dst, in_=src)

        def quantise_attn(r, q0, q1):
            if r not in a_codes:
                ac = keep.tile([P, Q], U32, tag="ac", align_bytes=64)
                asc = keep.tile([P, Q], U8, tag="asc", align_bytes=64)
                a_codes[r] = ac
                a_scales[r] = asc
            nc.vector.quantize_mx(
                out=a_codes[r][:, q0:q1].bitcast(FP8X4),
                scales=a_scales[r][:, q0:q1],
                in_=grouped[r][:, q0:q1, :].rearrange("p q t -> p (q t)"),
            )

        def mv_transposes(r, b):
            rawf = mvraw[r // 2][:].bitcast(F32)
            tp = psum.tile([P, 2, 2, P], F32, tag=("acc%d" % (2 * r + b) if r < 2 else "tp"))
            for jj in range(2):
                for u in range(2):
                    w0 = 256 * (r % 2) + 128 * u
                    nc.tensor.transpose(tp[:, jj, u, :], rawf[:, 2 * b + jj, w0 : w0 + 128], ident[:])
            tps[(r, b)] = tp

        def mv_copy(r, b):
            if r not in gmv:
                gm = work.tile([P, 4 * CV], BF16, tag="gmv", bufs=3, align_bytes=64)
                gmv[r] = gm
            words = gmv[r][:].bitcast(F32).rearrange("p (j c u) -> p j c u", j=4, u=2)
            nc.scalar.copy(out=words[:, 2 * b : 2 * b + 2], in_=tps[(r, b)][:].rearrange("p j u c -> p j c u"))

        def quantise_mv(r):
            vc = keep.tile([P, CV], U32, tag="vc", align_bytes=64)
            vs = keep.tile([P, CV], U8, tag="vs", align_bytes=64)
            nc.vector.quantize_mx(out=vc[:].bitcast(FP8X4), scales=vs[:], in_=gmv[r][:])
            v_codes[r] = vc
            v_scales[r] = vs

        def mx(n, h, g, j, tag):
            r = PASSES * n + g
            if g == 0:
                a = psum.tile([P, HALF], F32, tag=tag)
                acc[(n, h, j)] = a
            nc.tensor.matmul_mx(
                out=acc[(n, h, j)][:],
                lhsT=v_codes[r][:, P * j : P * j + P].bitcast(FP8X4),
                lhsT_scale=v_scales[r][:, P * j : P * j + P],
                rhs=a_codes[r][:, HALF * h : HALF * h + HALF].bitcast(FP8X4),
                rhs_scale=a_scales[r][:, HALF * h : HALF * h + HALF],
                start=(g == 0),
                stop=(g == PASSES - 1),
            )

        def leave(eng_name, n, h, j):
            if n == 0:
                ost = work.tile([P, HALF], F32, tag="ost", bufs=4)
                dst = ost[:]
            else:
                if (h, "end") not in acc:
                    big = raws.tile([P, 4, HALF], F32, tag="mvraw")
                    acc[(h, "end")] = big
                dst = acc[(h, "end")][:, j, :]
            if eng_name == "S":
                nc.scalar.copy(out=dst, in_=acc[(n, h, j)][:])
            else:
                nc.vector.tensor_copy(out=dst, in_=acc[(n, h, j)][:])
            stores["due"].append((out_v[n][:, 4 + j, HALF * h : HALF * h + HALF], dst))

        def cast_qv(eng_name, k):
            qvf = raws.tile([P, Q], F32, tag="qvf", bufs=8)
            if eng_name == "G":
                nc.gpsimd.tensor_scalar(out=qvf[:], in0=qv_b[k][:], scalar1=1.0, scalar2=0.0, op0=ALU.mult, op1=ALU.add)
            elif eng_name == "V":
                nc.vector.tensor_copy(out=qvf[:], in_=qv_b[k][:])
            else:
                nc.scalar.copy(out=qvf[:], in_=qv_b[k][:])
            stores["due"].append((out_v[k // 4][:, k % 4, :], qvf[:]))

        def flush_stores():
            for dst, src in stores["due"]:
                nc.sync.dma_start(out=dst, in_=src)
            stores["due"] = []

        def mx_plan(w):
            jobs = []
            if 2 <= w < 2 + PASSES:
                jobs.extend([(0, 0, w - 2, j, "acc%d" % j) for j in range(4)])
            if w in (10, 11):
                jobs.extend([(0, 1, g, j, "acc%d" % j) for j in (2 * (w - 10), 2 * (w - 10) + 1) for g in range(PASSES)])
            if w == 12:
                jobs.extend([(1, 0, g, j, "acc%d" % j) for g in range(3) for j in range(4)])
            if 13 <= w < ROUNDS:
                jobs.extend([(1, 0, w - 10, j, "acc%d" % j) for j in range(4)])
            plan = dict((k, []) for k in range(BANKS + 1))
            if w < LAST:
                early = max(0, len(jobs) - 10)
                for k in range(1, 7):
                    plan[k] = jobs[:early][k - 1 : k]
                plan[BANKS] = jobs[early:]
            else:
                jobs.extend([(1, 1, g, 0, "tp") for g in range(6)])
                for k in range(5):
                    plan[k] = jobs[2 * k : 2 * k + 2]
                for k, j, tag in ((5, 1, "ring2"), (6, 2, "ring0"), (7, 3, "ring1")):
                    plan[k] = [(1, 1, g, j, tag) for g in range(6)]
            return plan

        def mv_events(r):
            if r < LAST:
                return {7: (r + 1, 0), 9: (r + 1, 1)}
            return {}

        load_qk(0, 0)
        load_mk(0, 0, 1)
        load_qk(0, 1)
        for k in range(3):
            load_qv(k)
        load_mk(0, 1, 2)
        for k in range(3, 5):
            load_qv(k)
        load_mv(0)
        load_qv(5)
        load_mk(0, 2, 4)
        for c in range(RING):
            aff(c)
        for k in range(5):
            cast_qv("G", k)
        load_qv(6)
        load_qv(7)
        load_mv(1)

        for r in range(ROUNDS):
            if r == 0:
                load_mk(0, 4, 6)
                load_mk(0, 6, 8)
            if r % 2 == 1 and 2 <= (r + 3) // 2 < 8:
                load_mv((r + 3) // 2)
            if r == 3:
                load_qk(1, 0)
                load_qk(1, 1)
            if r in (3, 4, 5, 6):
                load_mk(1, 2 * (r - 3), 2 * (r - 3) + 2)

            plan = mx_plan(r)
            events = mv_events(r)
            for k in range(BANKS):
                c = BANKS * r + k
                shift_out(c)
                if c + RING < NAFF:
                    aff(c + RING)
                if r == 0 and k == 6:
                    mv_transposes(0, 0)
                    mv_transposes(0, 1)
                if k in events:
                    mv_transposes(*events[k])
                for job in plan[k]:
                    mx(*job)
                if k % 4 >= 2:
                    exp_tile(r, 2 * (k // 4) + k % 2)
                if r == 0 and k == 7:
                    mv_copy(0, 0)
                    mv_copy(0, 1)
                if k in events:
                    mv_copy(*events[k])
            for job in plan[BANKS]:
                mx(*job)
            if 9 in events:
                mv_transposes(*events[9])


            if r == 0:
                for k in range(5, 8):
                    cast_qv("V", k)
            if r >= 1:
                regroup("V", r - 1, GQ, GQ, Q)
            recip(r, 0)
            if r == 1:
                quantise_mv(0)
            if r >= 1:
                quantise_mv(r)
            if r == 9:
                leave("V", 0, 0, 0)
                leave("V", 0, 0, 1)
            if r in (10, 11):
                leave("V", 0, 1, 2 * (r - 10))
            if r >= 1:
                quantise_attn(r - 1, 0, Q)
            recip(r, 1)

            if r < LAST:
                direct(nc.gpsimd, r, 0, GQ)
            if r < LAST:
                stage(r, GQ, Q)
            if r == 9:
                leave("S", 0, 0, 2)
                leave("S", 0, 0, 3)
            if r in (10, 11):
                leave("S", 0, 1, 2 * (r - 10) + 1)
            if 9 in events:
                mv_copy(*events[9])
            flush_stores()

        stage(LAST, HALF, Q)
        for h in range(2):
            for j in range(4):
                mx(1, h, 6, j, "")
        direct(nc.vector, LAST, 0, HALF)
        regroup("S", LAST, HALF, Q - SREG, Q)
        quantise_attn(LAST, 0, HALF)
        regroup("V", LAST, HALF, HALF, Q - SREG)
        quantise_attn(LAST, HALF, Q)
        for j in range(4):
            mx(1, 0, 7, j, "")
        for j in range(4):
            leave("S" if j < 3 else "V", 1, 0, j)
        flush_stores()
        for j in range(4):
            mx(1, 1, 7, j, "")
        for j in range(4):
            leave("V" if j % 2 == 0 else "S", 1, 1, j)
        flush_stores()
